import numpy as np
import ml_dtypes


def mxq(x, axis, fmt="e4m3"):
    dtype, down = {"e4m3": (ml_dtypes.float8_e4m3fn, 7), "e5m2": (ml_dtypes.float8_e5m2, 14)}[fmt]
    v = np.moveaxis(np.asarray(x, np.float32).astype(ml_dtypes.bfloat16).astype(np.float64), axis, -1)
    blocks = v.reshape(v.shape[:-1] + (-1, 32))
    amax = np.abs(blocks).max(-1, keepdims=True)
    byte = np.maximum(np.where(amax > 0, np.frexp(amax)[1] - 1 + 127, 0) - down, 1)
    scale = np.exp2(byte - 127.0)
    codes = (blocks / scale).astype(np.float32).astype(dtype).astype(np.float64)
    return np.moveaxis((codes * scale).reshape(v.shape), -1, axis)


WIDE = False


def mx_kscale(k):
    if not WIDE:
        return np.ones(k)
    levels = np.array([10, -10, 5, -5, 0])
    a = np.random.permutation(np.resize(levels, k // 512 * 4)).reshape(k // 512, 4)
    idx = np.arange(k)
    return np.exp2(a[idx // 512, idx % 128 // 32])


BF16 = ml_dtypes.bfloat16


def bf(x):
    return np.asarray(x, np.float32).astype(BF16)


def f64(x):
    return np.asarray(x).astype(np.float64)


E2M1 = np.array([0.0, 0.5, 1.0, 1.5, 2.0, 3.0, 4.0, 6.0, -0.0, -0.5, -1.0, -1.5, -2.0, -3.0, -4.0, -6.0])


def pack_weight(w, fmt):
    k, n = w.shape
    w = f64(bf(w)).reshape(k // 32, 32, n)
    amax = np.abs(w).max(1)
    if fmt == "e4m3":
        byte = np.frexp(amax)[1] - 1 + 127 - 7
    else:
        mant, ex = np.frexp(amax / 6.0)
        byte = np.where(mant > 0.5, ex, ex - 1) + 127
    byte = np.clip(np.where(amax > 0, byte, 1), 1, 254)
    scaled = (w * np.exp2(127.0 - byte)[:, None, :]).reshape(k, n).astype(np.float32)
    by_word = np.ascontiguousarray(scaled.reshape(k // 512, 128, 4, n).transpose(0, 1, 3, 2))
    if fmt == "e4m3":
        words = by_word.astype(ml_dtypes.float8_e4m3fn).view(np.uint8)
    else:
        c = by_word.astype(ml_dtypes.float4_e2m1fn).view(np.uint8) & 0xF
        words = c[..., 0::2] | (c[..., 1::2] << 4)
    return np.ascontiguousarray(words), np.ascontiguousarray(byte.astype(np.uint8).reshape(k // 512, 16, n))


def unpack_weight(words, scales, fmt):
    g, p, n, _ = words.shape
    if fmt == "e4m3":
        vals = np.ascontiguousarray(words).view(ml_dtypes.float8_e4m3fn).astype(np.float64)
    else:
        nib = np.empty((g, p, n, 4), np.uint8)
        nib[..., 0::2] = words & 0xF
        nib[..., 1::2] = words >> 4
        vals = E2M1[nib]
    vals = vals * np.repeat(np.exp2(scales.astype(np.float64) - 127.0), 8, axis=1)[..., None]
    return vals.transpose(0, 1, 3, 2).reshape(g * 512, n)


B, I, H = 128, 2048, 1536
MXH = H % 512 == 0
FMT = "e4m3"


def sigmoid(v):
    return 1.0 / (1.0 + np.exp(-v))


def setup_inputs():
    s = mx_kscale(I)
    u = mx_kscale(H) if MXH else np.ones(H)
    d = {"x_t": bf(np.random.standard_normal((B, I)) * s),
         "h_prev": bf(np.random.standard_normal((B, H)) * u),
         "c_prev": bf(np.random.standard_normal((B, H)))}
    for g in ("f", "i", "c", "o"):
        words, scales = pack_weight(np.random.standard_normal((I, H)) * 0.7 / np.sqrt(I) / s[:, None], FMT)
        d["W_" + g + "_words"] = words
        d["W_" + g + "_scales"] = scales
    for g in ("f", "i", "c", "o"):
        words, scales = pack_weight(np.random.standard_normal((H, H)) * 0.7 / np.sqrt(H) / u[:, None], FMT)
        d["U_" + g + "_words"] = words
        d["U_" + g + "_scales"] = scales
    for g in ("f", "i", "c", "o"):
        d["b_" + g] = bf(np.random.standard_normal(H) * 0.1)
    return d


def reference(x_t, h_prev, c_prev, W_f_words, W_f_scales, W_i_words, W_i_scales, W_c_words, W_c_scales, W_o_words, W_o_scales, U_f_words, U_f_scales, U_i_words, U_i_scales, U_c_words, U_c_scales, U_o_words, U_o_scales, b_f, b_i, b_c, b_o):
    W = np.concatenate([unpack_weight(W_f_words, W_f_scales, FMT), unpack_weight(W_i_words, W_i_scales, FMT), unpack_weight(W_c_words, W_c_scales, FMT), unpack_weight(W_o_words, W_o_scales, FMT)], axis=1)
    U = np.concatenate([unpack_weight(U_f_words, U_f_scales, FMT), unpack_weight(U_i_words, U_i_scales, FMT), unpack_weight(U_c_words, U_c_scales, FMT), unpack_weight(U_o_words, U_o_scales, FMT)], axis=1)
    b = np.concatenate([f64(b_f), f64(b_i), f64(b_c), f64(b_o)], axis=0)
    xw = mxq(f64(x_t), 1, "e4m3") @ W
    if MXH:
        hu = mxq(f64(h_prev), 1, "e4m3") @ U
    else:
        hu = f64(h_prev) @ U
    gates = xw + hu + b
    f_t = sigmoid(gates[:, 0 * H:1 * H])
    i_t = sigmoid(gates[:, 1 * H:2 * H])
    c_tilda_t = np.tanh(gates[:, 2 * H:3 * H])
    o_t = sigmoid(gates[:, 3 * H:4 * H])
    c_t = f_t * f64(c_prev) + i_t * c_tilda_t
    h_t = o_t * np.tanh(c_t)
    return h_t

@@ -1,0 +1,158 @@
+from contextlib import ExitStack
+
+import concourse.mybir as mybir
+from concourse.masks import make_identity
+
+F32 = mybir.dt.float32
+BF16 = mybir.dt.bfloat16
+I32 = mybir.dt.int32
+U32 = mybir.dt.uint32
+U8 = mybir.dt.uint8
+FP8X4 = mybir.dt.float8_e4m3fn_x4
+ACT = mybir.ActivationFunctionType
+ALU = mybir.AluOpType
+
+P = 128
+I_DIM = 2048
+H = 1536
+K_PASS = 512
+GX = I_DIM // K_PASS
+GH = H // K_PASS
+G = GX + GH
+NT = 512
+NCH = H // NT
+WORD_BUFS = 16
+
+FLOPS = 2 * 128 * (I_DIM + H) * 4 * H
+
+
+def tile_lstmcell_w_kernel(
+    tc, x_t, h_prev, c_prev,
+    W_f_words, W_f_scales, W_i_words, W_i_scales, W_c_words, W_c_scales, W_o_words, W_o_scales,
+    U_f_words, U_f_scales, U_i_words, U_i_scales, U_c_words, U_c_scales, U_o_words, U_o_scales,
+    b_f, b_i, b_c, b_o, out,
+):
+    nc = tc.nc
+    w_words = [W_f_words, W_i_words, W_c_words, W_o_words]
+    w_scales = [W_f_scales, W_i_scales, W_c_scales, W_o_scales]
+    u_words = [U_f_words, U_i_words, U_c_words, U_o_words]
+    u_scales = [U_f_scales, U_i_scales, U_c_scales, U_o_scales]
+    biases = [b_f, b_i, b_c, b_o]
+    funcs = [ACT.Sigmoid, ACT.Sigmoid, ACT.Tanh, ACT.Sigmoid]
+
+    with ExitStack() as ctx:
+        keep = ctx.enter_context(tc.tile_pool(name="keep", bufs=1))
+        words = ctx.enter_context(tc.tile_pool(name="words", bufs=WORD_BUFS))
+        work = ctx.enter_context(tc.tile_pool(name="work", bufs=3))
+        psum = ctx.enter_context(tc.psum_pool(name="psum", bufs=8))
+
+        planes = keep.tile([P, 8 * H], U8, name="planes", align_bytes=64)
+        brow = keep.tile([P, 4 * H], BF16, name="brow")
+        ones = keep.tile([P, P], BF16, name="ones")
+        ident = keep.tile([P, P], F32, name="ident")
+        x_sb = keep.tile([P, I_DIM], BF16, name="x_sb")
+        h_sb = keep.tile([P, H], BF16, name="h_sb")
+        c_sb = keep.tile([P, H], BF16, name="c_sb")
+        grouped = keep.tile([P, G * K_PASS], BF16, name="grouped", align_bytes=64)
+        codes = keep.tile([P, G * P], U32, name="codes", align_bytes=64)
+        xplanes = keep.tile([P, G * P], U8, name="xplanes", align_bytes=64)
+        bias_bc = keep.tile([P, 4 * H], F32, name="bias_bc")
+        fc = keep.tile([P, H], F32, name="fc")
+        ig = keep.tile([P, H], F32, name="ig")
+        cg = keep.tile([P, H], F32, name="cg")
+        th = keep.tile([P, H], F32, name="th")
+
+        nc.sync.dma_start(out=x_sb[:], in_=x_t)
+        nc.sync.dma_start(out=h_sb[:], in_=h_prev)
+        nc.sync.dma_start(out=c_sb[:], in_=c_prev)
+        nc.vector.memset(planes[:].bitcast(I32), 0)
+        nc.vector.memset(brow[:].bitcast(I32), 0)
+        nc.vector.memset(ones[:], 1.0)
+        make_identity(nc, ident[:])
+        for gi in range(4):
+            nc.scalar.dma_start(out=brow[0:1, gi * H:(gi + 1) * H], in_=biases[gi].unsqueeze(0))
+
+        for gi in range(4):
+            for (sc, n_planes, base) in ((w_scales[gi], GX, gi * H), (u_scales[gi], GH, (4 + gi) * H)):
+                sc32 = sc.bitcast(I32)
+                for q in (0, 2, 1, 3):
+                    nc.sync.dma_start(
+                        out=planes[32 * q:32 * q + 4 * n_planes, base:base + H].bitcast(I32),
+                        in_=sc32[:, 4 * q:4 * q + 4, :],
+                    )
+
+        srcs = [(x_sb, g) for g in range(GX)] + [(h_sb, g) for g in range(GH)]
+        g32 = grouped[:].bitcast(F32)
+        for j in range((G + 1) // 2):
+            pair = srcs[2 * j:2 * j + 2]
+            n = len(pair)
+            xt = psum.tile([P, NT], F32, name="xt", tag="bank")
+            for a, (src, g) in enumerate(pair):
+                s32 = src[:].bitcast(F32)
+                for u in range(2):
+                    nc.tensor.transpose(
+                        xt[:, (2 * a + u) * P:(2 * a + u + 1) * P],
+                        s32[:, 256 * g + u:256 * (g + 1):2],
+                        ident[:],
+                    )
+            dst = g32[:, 512 * j:512 * j + 256 * n].rearrange("p (a b u) -> p a b u", a=n, u=2)
+            srcv = xt[:, 0:256 * n].rearrange("p (a u b) -> p a b u", a=n, u=2)
+            if j % 2 == 0:
+                nc.vector.tensor_copy(out=dst, in_=srcv)
+            else:
+                nc.scalar.copy(out=dst, in_=srcv)
+        for (lo, width) in ((0, 2048), (2048, 1024), (3072, 512)):
+            nc.vector.quantize_mx(
+                out=codes[:, lo // 4:(lo + width) // 4].bitcast(FP8X4),
+                scales=xplanes[:, lo // 4:(lo + width) // 4],
+                in_=grouped[:, lo:lo + width],
+            )
+
+        for cb in range(4 * NCH):
+            bp = psum.tile([P, NT], F32, name="bp", tag="bank")
+            nc.tensor.matmul(out=bp[:], lhsT=ones[:], rhs=brow[:, cb * NT:(cb + 1) * NT], start=True, stop=True)
+            nc.scalar.copy(out=bias_bc[:, cb * NT:(cb + 1) * NT], in_=bp[:])
+
+        for gi in range(4):
+            accs = [psum.tile([P, NT], F32, name="acc%d" % c, tag="bank") for c in range(NCH)]
+            for g in range(G):
+                wt = words.tile([P, H], U32, name="wt", tag="wt", align_bytes=64)
+                if g < GX:
+                    src_w = w_words[gi][g]
+                    k = 4 * g
+                    base = gi * H
+                else:
+                    src_w = u_words[gi][g - GX]
+                    k = 4 * (g - GX)
+                    base = (4 + gi) * H
+                nc.sync.dma_start(out=wt[:].bitcast(I32), in_=src_w.rearrange("p n t -> p (n t)").bitcast(I32))
+                for c in range(NCH):
+                    nc.tensor.matmul_mx(
+                        out=accs[c][:],
+                        lhsT=codes[:, g * P:(g + 1) * P].bitcast(FP8X4),
+                        lhsT_scale=xplanes[:, g * P:(g + 1) * P],
+                        rhs=wt[:, c * NT:(c + 1) * NT].bitcast(FP8X4),
+                        rhs_scale=planes[k:P, base + c * NT:base + (c + 1) * NT],
+                        start=(g == 0),
+                        stop=(g == G - 1),
+                    )
+            for c in range(NCH):
+                cols = slice(c * NT, (c + 1) * NT)
+                z = work.tile([P, NT], F32, name="z", tag="z")
+                nc.vector.tensor_tensor(out=z[:], in0=accs[c][:], in1=bias_bc[:, gi * H + c * NT:gi * H + (c + 1) * NT], op=ALU.add)
+                if gi == 0:
+                    nc.scalar.activation(out=fc[:, cols], in_=z[:], func=funcs[gi])
+                    nc.vector.tensor_tensor(out=fc[:, cols], in0=fc[:, cols], in1=c_sb[:, cols], op=ALU.mult)
+                elif gi == 1:
+                    nc.scalar.activation(out=ig[:, cols], in_=z[:], func=funcs[gi])
+                elif gi == 2:
+                    nc.scalar.activation(out=cg[:, cols], in_=z[:], func=funcs[gi])
+                    nc.vector.tensor_tensor(out=cg[:, cols], in0=cg[:, cols], in1=ig[:, cols], op=ALU.mult)
+                    nc.vector.tensor_tensor(out=cg[:, cols], in0=cg[:, cols], in1=fc[:, cols], op=ALU.add)
+                    nc.scalar.activation(out=th[:, cols], in_=cg[:, cols], func=ACT.Tanh)
+                else:
+                    og = work.tile([P, NT], F32, name="og", tag="og")
+                    nc.scalar.activation(out=og[:], in_=z[:], func=funcs[gi])
+                    res = work.tile([P, NT], F32, name="res", tag="res")
+                    nc.vector.tensor_tensor(out=res[:], in0=og[:], in1=th[:, cols], op=ALU.mult)
+                    nc.sync.dma_start(out=out[:, cols], in_=res[:])

@@ -45,6 +45,7 @@ def tile_lstmcell_w_kernel(
         words = ctx.enter_context(tc.tile_pool(name="words", bufs=WORD_BUFS))
         work = ctx.enter_context(tc.tile_pool(name="work", bufs=3))
         psum = ctx.enter_context(tc.psum_pool(name="psum", bufs=8))
+        ctx.enter_context(tc.manual_schedule())
 
         planes = keep.tile([P, 8 * H], U8, name="planes", align_bytes=64)
         brow = keep.tile([P, 4 * H], BF16, name="brow")
@@ -64,22 +65,35 @@ def tile_lstmcell_w_kernel(
 
         nc.sync.dma_start(out=x_sb[:], in_=x_t)
         nc.sync.dma_start(out=h_sb[:], in_=h_prev)
-        nc.sync.dma_start(out=c_sb[:], in_=c_prev)
-        nc.vector.memset(planes[:].bitcast(I32), 0)
+        for gi in range(4):
+            nc.vector.memset(planes[:, 2 * gi * H:2 * (gi + 1) * H].bitcast(I32), 0)
         nc.vector.memset(brow[:].bitcast(I32), 0)
         nc.vector.memset(ones[:], 1.0)
         make_identity(nc, ident[:])
-        for gi in range(4):
-            nc.scalar.dma_start(out=brow[0:1, gi * H:(gi + 1) * H], in_=biases[gi].unsqueeze(0))
 
         for gi in range(4):
-            for (sc, n_planes, base) in ((w_scales[gi], GX, gi * H), (u_scales[gi], GH, (4 + gi) * H)):
-                sc32 = sc.bitcast(I32)
+            for (sc, n_planes, base) in ((w_scales[gi], GX, 2 * gi * H), (u_scales[gi], GH, (2 * gi + 1) * H)):
+                scf = sc.bitcast(F32)
                 for q in (0, 2, 1, 3):
-                    nc.sync.dma_start(
-                        out=planes[32 * q:32 * q + 4 * n_planes, base:base + H].bitcast(I32),
-                        in_=sc32[:, 4 * q:4 * q + 4, :],
+                    nc.gpsimd.dma_start(
+                        out=planes[32 * q:32 * q + 4 * n_planes, base:base + H].bitcast(F32),
+                        in_=scf[:, 4 * q:4 * q + 4, :],
                     )
+
+        order = [(gi, g) for gi in range(4) for g in range(G)]
+        wts = {}
+
+        def load_words(j):
+            gi, g = order[j]
+            wt = words.tile([P, H], U32, name="wt", tag="wt", align_bytes=64)
+            src_w = w_words[gi][g] if g < GX else u_words[gi][g - GX]
+            nc.sync.dma_start(out=wt[:].bitcast(I32), in_=src_w.rearrange("p n t -> p (n t)").bitcast(I32))
+            wts[j] = wt
+
+        for j in range(WORD_BUFS):
+            load_words(j)
+            if j == 3:
+                nc.sync.dma_start(out=c_sb[:], in_=c_prev)
 
         srcs = [(x_sb, g) for g in range(GX)] + [(h_sb, g) for g in range(GH)]
         g32 = grouped[:].bitcast(F32)
@@ -101,6 +115,8 @@ def tile_lstmcell_w_kernel(
                 nc.vector.tensor_copy(out=dst, in_=srcv)
             else:
                 nc.scalar.copy(out=dst, in_=srcv)
+        for gi in range(4):
+            nc.scalar.dma_start(out=brow[0:1, gi * H:(gi + 1) * H], in_=biases[gi].unsqueeze(0))
         for (lo, width) in ((0, 2048), (2048, 1024), (3072, 512)):
             nc.vector.quantize_mx(
                 out=codes[:, lo // 4:(lo + width) // 4].bitcast(FP8X4),
@@ -111,21 +127,22 @@ def tile_lstmcell_w_kernel(
         for cb in range(4 * NCH):
             bp = psum.tile([P, NT], F32, name="bp", tag="bank")
             nc.tensor.matmul(out=bp[:], lhsT=ones[:], rhs=brow[:, cb * NT:(cb + 1) * NT], start=True, stop=True)
-            nc.scalar.copy(out=bias_bc[:, cb * NT:(cb + 1) * NT], in_=bp[:])
+            if cb % 2 == 0:
+                nc.scalar.copy(out=bias_bc[:, cb * NT:(cb + 1) * NT], in_=bp[:])
+            else:
+                nc.vector.tensor_copy(out=bias_bc[:, cb * NT:(cb + 1) * NT], in_=bp[:])
 
         for gi in range(4):
             accs = [psum.tile([P, NT], F32, name="acc%d" % c, tag="bank") for c in range(NCH)]
             for g in range(G):
-                wt = words.tile([P, H], U32, name="wt", tag="wt", align_bytes=64)
+                j = gi * G + g
+                wt = wts[j]
                 if g < GX:
-                    src_w = w_words[gi][g]
                     k = 4 * g
-                    base = gi * H
+                    base = 2 * gi * H
                 else:
-                    src_w = u_words[gi][g - GX]
                     k = 4 * (g - GX)
-                    base = (4 + gi) * H
-                nc.sync.dma_start(out=wt[:].bitcast(I32), in_=src_w.rearrange("p n t -> p (n t)").bitcast(I32))
+                    base = (2 * gi + 1) * H
                 for c in range(NCH):
                     nc.tensor.matmul_mx(
                         out=accs[c][:],
@@ -136,23 +153,29 @@ def tile_lstmcell_w_kernel(
                         start=(g == 0),
                         stop=(g == G - 1),
                     )
+                if j + WORD_BUFS < len(order):
+                    load_words(j + WORD_BUFS)
+            dsts = [fc, ig, cg, None]
+            ogs = []
             for c in range(NCH):
                 cols = slice(c * NT, (c + 1) * NT)
                 z = work.tile([P, NT], F32, name="z", tag="z")
                 nc.vector.tensor_tensor(out=z[:], in0=accs[c][:], in1=bias_bc[:, gi * H + c * NT:gi * H + (c + 1) * NT], op=ALU.add)
-                if gi == 0:
-                    nc.scalar.activation(out=fc[:, cols], in_=z[:], func=funcs[gi])
-                    nc.vector.tensor_tensor(out=fc[:, cols], in0=fc[:, cols], in1=c_sb[:, cols], op=ALU.mult)
-                elif gi == 1:
-                    nc.scalar.activation(out=ig[:, cols], in_=z[:], func=funcs[gi])
-                elif gi == 2:
-                    nc.scalar.activation(out=cg[:, cols], in_=z[:], func=funcs[gi])
-                    nc.vector.tensor_tensor(out=cg[:, cols], in0=cg[:, cols], in1=ig[:, cols], op=ALU.mult)
-                    nc.vector.tensor_tensor(out=cg[:, cols], in0=cg[:, cols], in1=fc[:, cols], op=ALU.add)
-                    nc.scalar.activation(out=th[:, cols], in_=cg[:, cols], func=ACT.Tanh)
+                if gi < 3:
+                    nc.scalar.activation(out=dsts[gi][:, cols], in_=z[:], func=funcs[gi])
                 else:
                     og = work.tile([P, NT], F32, name="og", tag="og")
                     nc.scalar.activation(out=og[:], in_=z[:], func=funcs[gi])
+                    ogs.append(og)
+            for c in range(NCH):
+                cols = slice(c * NT, (c + 1) * NT)
+                if gi == 0:
+                    nc.vector.tensor_tensor(out=fc[:, cols], in0=fc[:, cols], in1=c_sb[:, cols], op=ALU.mult)
+                elif gi == 2:
+                    nc.vector.tensor_tensor(out=cg[:, cols], in0=cg[:, cols], in1=ig[:, cols], op=ALU.mult)
+                    nc.vector.tensor_tensor(out=cg[:, cols], in0=cg[:, cols], in1=fc[:, cols], op=ALU.add)
+                    nc.scalar.activation(out=th[:, cols], in_=cg[:, cols], func=ACT.Tanh)
+                elif gi == 3:
                     res = work.tile([P, NT], F32, name="res", tag="res")
-                    nc.vector.tensor_tensor(out=res[:], in0=og[:], in1=th[:, cols], op=ALU.mult)
+                    nc.vector.tensor_tensor(out=res[:], in0=ogs[c][:], in1=th[:, cols], op=ALU.mult)
                     nc.sync.dma_start(out=out[:, cols], in_=res[:])

@@ -63,22 +63,25 @@ def tile_lstmcell_w_kernel(
         cg = keep.tile([P, H], F32, name="cg")
         th = keep.tile([P, H], F32, name="th")
 
-        nc.sync.dma_start(out=x_sb[:], in_=x_t)
-        nc.sync.dma_start(out=h_sb[:], in_=h_prev)
-        for gi in range(4):
-            nc.vector.memset(planes[:, 2 * gi * H:2 * (gi + 1) * H].bitcast(I32), 0)
+        blocks = {("w", 0): 0, ("w", 1): 1, ("u", 0): 2, ("u", 1): 3, ("w", 2): 4, ("u", 2): 5, ("w", 3): 6, ("u", 3): 7}
+        for piece in range(4):
+            nc.vector.memset(planes[:, 2 * piece * H:2 * (piece + 1) * H].bitcast(I32), 0)
         nc.vector.memset(brow[:].bitcast(I32), 0)
         nc.vector.memset(ones[:], 1.0)
         make_identity(nc, ident[:])
 
-        for gi in range(4):
-            for (sc, n_planes, base) in ((w_scales[gi], GX, 2 * gi * H), (u_scales[gi], GH, (2 * gi + 1) * H)):
-                scf = sc.bitcast(F32)
-                for q in (0, 2, 1, 3):
-                    nc.gpsimd.dma_start(
-                        out=planes[32 * q:32 * q + 4 * n_planes, base:base + H].bitcast(F32),
-                        in_=scf[:, 4 * q:4 * q + 4, :],
-                    )
+        def load_scales(kind, gi, engine, dt):
+            sc = (w_scales[gi] if kind == "w" else u_scales[gi]).bitcast(dt)
+            n_planes = GX if kind == "w" else GH
+            base = blocks[(kind, gi)] * H
+            for q in (0, 2, 1, 3):
+                engine.dma_start(
+                    out=planes[32 * q:32 * q + 4 * n_planes, base:base + H].bitcast(dt),
+                    in_=sc[:, 4 * q:4 * q + 4, :],
+                )
+
+        for (kind, gi) in (("u", 0), ("u", 1), ("w", 2), ("u", 2), ("w", 3), ("u", 3)):
+            load_scales(kind, gi, nc.gpsimd, F32)
 
         order = [(gi, g) for gi in range(4) for g in range(G)]
         wts = {}
@@ -90,10 +93,14 @@ def tile_lstmcell_w_kernel(
             nc.sync.dma_start(out=wt[:].bitcast(I32), in_=src_w.rearrange("p n t -> p (n t)").bitcast(I32))
             wts[j] = wt
 
+        nc.sync.dma_start(out=x_sb[:], in_=x_t)
+        load_scales("w", 0, nc.sync, I32)
+        nc.sync.dma_start(out=h_sb[:], in_=h_prev)
         for j in range(WORD_BUFS):
             load_words(j)
             if j == 3:
                 nc.sync.dma_start(out=c_sb[:], in_=c_prev)
+                load_scales("w", 1, nc.sync, I32)
 
         srcs = [(x_sb, g) for g in range(GX)] + [(h_sb, g) for g in range(GH)]
         g32 = grouped[:].bitcast(F32)
@@ -139,10 +146,10 @@ def tile_lstmcell_w_kernel(
                 wt = wts[j]
                 if g < GX:
                     k = 4 * g
-                    base = 2 * gi * H
+                    base = blocks[("w", gi)] * H
                 else:
                     k = 4 * (g - GX)
-                    base = (2 * gi + 1) * H
+                    base = blocks[("u", gi)] * H
                 for c in range(NCH):
                     nc.tensor.matmul_mx(
                         out=accs[c][:],

@@ -63,7 +63,7 @@ def tile_lstmcell_w_kernel(
         cg = keep.tile([P, H], F32, name="cg")
         th = keep.tile([P, H], F32, name="th")
 
-        blocks = {("w", 0): 0, ("w", 1): 1, ("u", 0): 2, ("u", 1): 3, ("w", 2): 4, ("u", 2): 5, ("w", 3): 6, ("u", 3): 7}
+        blocks = {("w", 0): 0, ("u", 0): 1, ("w", 1): 2, ("u", 1): 3, ("w", 2): 4, ("u", 2): 5, ("w", 3): 6, ("u", 3): 7}
         for piece in range(4):
             nc.vector.memset(planes[:, 2 * piece * H:2 * (piece + 1) * H].bitcast(I32), 0)
         nc.vector.memset(brow[:].bitcast(I32), 0)
@@ -80,17 +80,34 @@ def tile_lstmcell_w_kernel(
                     in_=sc[:, 4 * q:4 * q + 4, :],
                 )
 
-        for (kind, gi) in (("u", 0), ("u", 1), ("w", 2), ("u", 2), ("w", 3), ("u", 3)):
-            load_scales(kind, gi, nc.gpsimd, F32)
+        for gi in range(4):
+            load_scales("u", gi, nc.gpsimd, F32)
 
-        order = [(gi, g) for gi in range(4) for g in range(G)]
+        units = []
+        for gi in range(4):
+            for g in range(G):
+                if gi < 3 or g < GX:
+                    units.append((gi, (g,), 0, H))
+        gate_parts = [[(c * NT, NT) for c in range(NCH)] for gi in range(3)] + [[(0, 512), (512, 512), (1024, 256), (1280, 256)]]
+        for (p0, pn) in gate_parts[3]:
+            units.append((3, (4, 5, 6), p0, pn))
         wts = {}
 
         def load_words(j):
-            gi, g = order[j]
+            gi, gs, lo, n = units[j]
             wt = words.tile([P, H], U32, name="wt", tag="wt", align_bytes=64)
-            src_w = w_words[gi][g] if g < GX else u_words[gi][g - GX]
-            nc.sync.dma_start(out=wt[:].bitcast(I32), in_=src_w.rearrange("p n t -> p (n t)").bitcast(I32))
+            if len(gs) == 1:
+                g = gs[0]
+                src_w = w_words[gi][g] if g < GX else u_words[gi][g - GX]
+                nc.sync.dma_start(
+                    out=wt[:, 0:n].bitcast(I32),
+                    in_=src_w.rearrange("p n t -> p (n t)")[:, 4 * lo:4 * (lo + n)].bitcast(I32),
+                )
+            else:
+                nc.sync.dma_start(
+                    out=wt[:, 0:len(gs) * n].bitcast(I32).rearrange("p (g n) -> p g n", g=len(gs)),
+                    in_=u_words[gi].rearrange("g p n t -> p g (n t)")[:, :, 4 * lo:4 * (lo + n)].bitcast(I32),
+                )
             wts[j] = wt
 
         nc.sync.dma_start(out=x_sb[:], in_=x_t)
@@ -100,7 +117,8 @@ def tile_lstmcell_w_kernel(
             load_words(j)
             if j == 3:
                 nc.sync.dma_start(out=c_sb[:], in_=c_prev)
-                load_scales("w", 1, nc.sync, I32)
+            if j % 4 == 3 and j < 12:
+                load_scales("w", j // 4 + 1, nc.sync, I32)
 
         srcs = [(x_sb, g) for g in range(GX)] + [(h_sb, g) for g in range(GH)]
         g32 = grouped[:].bitcast(F32)
@@ -139,50 +157,67 @@ def tile_lstmcell_w_kernel(
             else:
                 nc.vector.tensor_copy(out=bias_bc[:, cb * NT:(cb + 1) * NT], in_=bp[:])
 
-        for gi in range(4):
-            accs = [psum.tile([P, NT], F32, name="acc%d" % c, tag="bank") for c in range(NCH)]
-            for g in range(G):
-                j = gi * G + g
-                wt = wts[j]
+        dsts = [fc, ig, cg, None]
+
+        def pre_activation(gi, acc, lo, n):
+            z = work.tile([P, NT], F32, name="z", tag="z")
+            nc.vector.tensor_tensor(out=z[:, 0:n], in0=acc, in1=bias_bc[:, gi * H + lo:gi * H + lo + n], op=ALU.add)
+            if gi < 3:
+                nc.scalar.activation(out=dsts[gi][:, lo:lo + n], in_=z[:, 0:n], func=funcs[gi])
+                return None
+            og = work.tile([P, NT], F32, name="og", tag="og")
+            nc.scalar.activation(out=og[:, 0:n], in_=z[:, 0:n], func=funcs[gi])
+            return og
+
+        def combine(gi, og, lo, n):
+            cols = slice(lo, lo + n)
+            if gi == 0:
+                nc.vector.tensor_tensor(out=fc[:, cols], in0=fc[:, cols], in1=c_sb[:, cols], op=ALU.mult)
+            elif gi == 2:
+                nc.vector.tensor_tensor(out=cg[:, cols], in0=cg[:, cols], in1=ig[:, cols], op=ALU.mult)
+                nc.vector.tensor_tensor(out=cg[:, cols], in0=cg[:, cols], in1=fc[:, cols], op=ALU.add)
+                nc.scalar.activation(out=th[:, cols], in_=cg[:, cols], func=ACT.Tanh)
+            elif gi == 3:
+                res = work.tile([P, NT], F32, name="res", tag="res")
+                nc.vector.tensor_tensor(out=res[:, 0:n], in0=og[:, 0:n], in1=th[:, cols], op=ALU.mult)
+                nc.sync.dma_start(out=out[:, cols], in_=res[:, 0:n])
+
+        accs = {}
+        waiting = []
+        n_done = 0
+        for j, (gi, gs, lo, n) in enumerate(units):
+            if gs[0] == 0:
+                for (p0, pn) in gate_parts[gi]:
+                    accs[(gi, p0)] = psum.tile([P, NT], F32, name="acc%d" % p0, tag="bank")
+            wt = wts[j]
+            mine = [(p0, pn) for (p0, pn) in gate_parts[gi] if lo <= p0 < lo + n]
+            for a, g in enumerate(gs):
                 if g < GX:
                     k = 4 * g
                     base = blocks[("w", gi)] * H
                 else:
                     k = 4 * (g - GX)
                     base = blocks[("u", gi)] * H
-                for c in range(NCH):
+                for (p0, pn) in mine:
+                    off = a * n + p0 - lo
                     nc.tensor.matmul_mx(
-                        out=accs[c][:],
+                        out=accs[(gi, p0)][:, 0:pn],
                         lhsT=codes[:, g * P:(g + 1) * P].bitcast(FP8X4),
                         lhsT_scale=xplanes[:, g * P:(g + 1) * P],
-                        rhs=wt[:, c * NT:(c + 1) * NT].bitcast(FP8X4),
-                        rhs_scale=planes[k:P, base + c * NT:base + (c + 1) * NT],
+                        rhs=wt[:, off:off + pn].bitcast(FP8X4),
+                        rhs_scale=planes[k:P, base + p0:base + p0 + pn],
                         start=(g == 0),
                         stop=(g == G - 1),
                     )
-                if j + WORD_BUFS < len(order):
-                    load_words(j + WORD_BUFS)
-            dsts = [fc, ig, cg, None]
-            ogs = []
-            for c in range(NCH):
-                cols = slice(c * NT, (c + 1) * NT)
-                z = work.tile([P, NT], F32, name="z", tag="z")
-                nc.vector.tensor_tensor(out=z[:], in0=accs[c][:], in1=bias_bc[:, gi * H + c * NT:gi * H + (c + 1) * NT], op=ALU.add)
-                if gi < 3:
-                    nc.scalar.activation(out=dsts[gi][:, cols], in_=z[:], func=funcs[gi])
-                else:
-                    og = work.tile([P, NT], F32, name="og", tag="og")
-                    nc.scalar.activation(out=og[:], in_=z[:], func=funcs[gi])
-                    ogs.append(og)
-            for c in range(NCH):
-                cols = slice(c * NT, (c + 1) * NT)
-                if gi == 0:
-                    nc.vector.tensor_tensor(out=fc[:, cols], in0=fc[:, cols], in1=c_sb[:, cols], op=ALU.mult)
-                elif gi == 2:
-                    nc.vector.tensor_tensor(out=cg[:, cols], in0=cg[:, cols], in1=ig[:, cols], op=ALU.mult)
-                    nc.vector.tensor_tensor(out=cg[:, cols], in0=cg[:, cols], in1=fc[:, cols], op=ALU.add)
-                    nc.scalar.activation(out=th[:, cols], in_=cg[:, cols], func=ACT.Tanh)
-                elif gi == 3:
-                    res = work.tile([P, NT], F32, name="res", tag="res")
-                    nc.vector.tensor_tensor(out=res[:], in0=ogs[c][:], in1=th[:, cols], op=ALU.mult)
-                    nc.sync.dma_start(out=out[:, cols], in_=res[:])
+            if j + WORD_BUFS < len(units):
+                load_words(j + WORD_BUFS)
+            if gs[-1] == G - 1:
+                for (p0, pn) in mine:
+                    waiting.append((pre_activation(gi, accs[(gi, p0)][:, 0:pn], p0, pn), p0, pn))
+                keep_back = 0
+                if gi == 3 and 0 < mine[0][0] and j < len(units) - 1:
+                    keep_back = 1 if mine[0][0] > 512 else 2
+                while n_done < len(waiting) - keep_back:
+                    og, p0, pn = waiting[n_done]
+                    combine(gi, og, p0, pn)
+                    n_done += 1

@@ -66,7 +66,6 @@ def tile_lstmcell_w_kernel(
         blocks = {("w", 0): 0, ("u", 0): 1, ("w", 1): 2, ("u", 1): 3, ("w", 2): 4, ("u", 2): 5, ("w", 3): 6, ("u", 3): 7}
         for piece in range(4):
             nc.vector.memset(planes[:, 2 * piece * H:2 * (piece + 1) * H].bitcast(I32), 0)
-        nc.vector.memset(brow[:].bitcast(I32), 0)
         nc.vector.memset(ones[:], 1.0)
         make_identity(nc, ident[:])
 
@@ -80,8 +79,8 @@ def tile_lstmcell_w_kernel(
                     in_=sc[:, 4 * q:4 * q + 4, :],
                 )
 
-        for gi in range(4):
-            load_scales("u", gi, nc.gpsimd, F32)
+        for (kind, gi) in (("u", 0), ("w", 1), ("u", 1), ("w", 2), ("u", 2), ("w", 3), ("u", 3)):
+            load_scales(kind, gi, nc.gpsimd, F32)
 
         units = []
         for gi in range(4):
@@ -117,8 +116,6 @@ def tile_lstmcell_w_kernel(
             load_words(j)
             if j == 3:
                 nc.sync.dma_start(out=c_sb[:], in_=c_prev)
-            if j % 4 == 3 and j < 12:
-                load_scales("w", j // 4 + 1, nc.sync, I32)
 
         srcs = [(x_sb, g) for g in range(GX)] + [(h_sb, g) for g in range(GH)]
         g32 = grouped[:].bitcast(F32)
@@ -140,22 +137,24 @@ def tile_lstmcell_w_kernel(
                 nc.vector.tensor_copy(out=dst, in_=srcv)
             else:
                 nc.scalar.copy(out=dst, in_=srcv)
-        for gi in range(4):
-            nc.scalar.dma_start(out=brow[0:1, gi * H:(gi + 1) * H], in_=biases[gi].unsqueeze(0))
         for (lo, width) in ((0, 2048), (2048, 1024), (3072, 512)):
             nc.vector.quantize_mx(
                 out=codes[:, lo // 4:(lo + width) // 4].bitcast(FP8X4),
                 scales=xplanes[:, lo // 4:(lo + width) // 4],
                 in_=grouped[:, lo:lo + width],
             )
+        nc.vector.memset(brow[:].bitcast(I32), 0)
+        for gi in range(4):
+            nc.scalar.dma_start(out=brow[0:1, gi * H:(gi + 1) * H], in_=biases[gi].unsqueeze(0))
 
-        for cb in range(4 * NCH):
-            bp = psum.tile([P, NT], F32, name="bp", tag="bank")
-            nc.tensor.matmul(out=bp[:], lhsT=ones[:], rhs=brow[:, cb * NT:(cb + 1) * NT], start=True, stop=True)
-            if cb % 2 == 0:
-                nc.scalar.copy(out=bias_bc[:, cb * NT:(cb + 1) * NT], in_=bp[:])
-            else:
-                nc.vector.tensor_copy(out=bias_bc[:, cb * NT:(cb + 1) * NT], in_=bp[:])
+        def spread_bias(gi):
+            for cb in range(gi * NCH, (gi + 1) * NCH):
+                bp = psum.tile([P, NT], F32, name="bp", tag="bank")
+                nc.tensor.matmul(out=bp[:], lhsT=ones[:], rhs=brow[:, cb * NT:(cb + 1) * NT], start=True, stop=True)
+                if cb % 2 == 0:
+                    nc.scalar.copy(out=bias_bc[:, cb * NT:(cb + 1) * NT], in_=bp[:])
+                else:
+                    nc.vector.tensor_copy(out=bias_bc[:, cb * NT:(cb + 1) * NT], in_=bp[:])
 
         dsts = [fc, ig, cg, None]
 
@@ -211,6 +210,8 @@ def tile_lstmcell_w_kernel(
                     )
             if j + WORD_BUFS < len(units):
                 load_words(j + WORD_BUFS)
+            if gs[0] == (4 if gi < 3 else 2) and lo == 0:
+                spread_bias(gi)
             if gs[-1] == G - 1:
                 for (p0, pn) in mine:
                     waiting.append((pre_activation(gi, accs[(gi, p0)][:, 0:pn], p0, pn), p0, pn))

@@ -22,6 +22,7 @@ G = GX + GH
 NT = 512
 NCH = H // NT
 WORD_BUFS = 16
+LOOKAHEAD = 8
 
 FLOPS = 2 * 128 * (I_DIM + H) * 4 * H
 
@@ -79,7 +80,7 @@ def tile_lstmcell_w_kernel(
                     in_=sc[:, 4 * q:4 * q + 4, :],
                 )
 
-        for (kind, gi) in (("u", 0), ("w", 1), ("u", 1), ("w", 2), ("u", 2), ("w", 3), ("u", 3)):
+        for (kind, gi) in (("u", 0), ("u", 1), ("u", 2), ("w", 3), ("u", 3)):
             load_scales(kind, gi, nc.gpsimd, F32)
 
         units = []
@@ -98,10 +99,16 @@ def tile_lstmcell_w_kernel(
             if len(gs) == 1:
                 g = gs[0]
                 src_w = w_words[gi][g] if g < GX else u_words[gi][g - GX]
-                nc.sync.dma_start(
-                    out=wt[:, 0:n].bitcast(I32),
-                    in_=src_w.rearrange("p n t -> p (n t)")[:, 4 * lo:4 * (lo + n)].bitcast(I32),
-                )
+                if j % 2 == 0 or j < LOOKAHEAD:
+                    nc.sync.dma_start(
+                        out=wt[:, 0:n].bitcast(I32),
+                        in_=src_w.rearrange("p n t -> p (n t)")[:, 4 * lo:4 * (lo + n)].bitcast(I32),
+                    )
+                else:
+                    nc.scalar.dma_start(
+                        out=wt[:, 0:n].bitcast(F32),
+                        in_=src_w.rearrange("p n t -> p (n t)")[:, 4 * lo:4 * (lo + n)].bitcast(F32),
+                    )
             else:
                 nc.sync.dma_start(
                     out=wt[:, 0:len(gs) * n].bitcast(I32).rearrange("p (g n) -> p g n", g=len(gs)),
@@ -112,10 +119,15 @@ def tile_lstmcell_w_kernel(
         nc.sync.dma_start(out=x_sb[:], in_=x_t)
         load_scales("w", 0, nc.sync, I32)
         nc.sync.dma_start(out=h_sb[:], in_=h_prev)
-        for j in range(WORD_BUFS):
-            load_words(j)
-            if j == 3:
-                nc.sync.dma_start(out=c_sb[:], in_=c_prev)
+        def first_loads(j0, j1):
+            for j in range(j0, j1):
+                load_words(j)
+                if j == 3:
+                    nc.sync.dma_start(out=c_sb[:], in_=c_prev)
+                if j in (3, 7):
+                    load_scales("w", (j + 1) // 4, nc.sync, I32)
+
+        first_loads(0, LOOKAHEAD)
 
         srcs = [(x_sb, g) for g in range(GX)] + [(h_sb, g) for g in range(GH)]
         g32 = grouped[:].bitcast(F32)
@@ -208,8 +220,8 @@ def tile_lstmcell_w_kernel(
                         start=(g == 0),
                         stop=(g == G - 1),
                     )
-            if j + WORD_BUFS < len(units):
-                load_words(j + WORD_BUFS)
+            if j + LOOKAHEAD < len(units):
+                load_words(j + LOOKAHEAD)
             if gs[0] == (4 if gi < 3 else 2) and lo == 0:
                 spread_bias(gi)
             if gs[-1] == G - 1:

@@ -44,7 +44,7 @@ def tile_lstmcell_w_kernel(
     with ExitStack() as ctx:
         keep = ctx.enter_context(tc.tile_pool(name="keep", bufs=1))
         words = ctx.enter_context(tc.tile_pool(name="words", bufs=WORD_BUFS))
-        work = ctx.enter_context(tc.tile_pool(name="work", bufs=3))
+        work = ctx.enter_context(tc.tile_pool(name="work", bufs=5))
         psum = ctx.enter_context(tc.psum_pool(name="psum", bufs=8))
         ctx.enter_context(tc.manual_schedule())
 
@@ -88,7 +88,7 @@ def tile_lstmcell_w_kernel(
             for g in range(G):
                 if gi < 3 or g < GX:
                     units.append((gi, (g,), 0, H))
-        gate_parts = [[(c * NT, NT) for c in range(NCH)] for gi in range(3)] + [[(0, 512), (512, 512), (1024, 256), (1280, 256)]]
+        gate_parts = [[(c * NT, NT) for c in range(NCH)] for gi in range(3)] + [[(0, 512), (512, 512), (1024, 256), (1280, 128), (1408, 128)]]
         for (p0, pn) in gate_parts[3]:
             units.append((3, (4, 5, 6), p0, pn))
         wts = {}
@@ -227,9 +227,7 @@ def tile_lstmcell_w_kernel(
             if gs[-1] == G - 1:
                 for (p0, pn) in mine:
                     waiting.append((pre_activation(gi, accs[(gi, p0)][:, 0:pn], p0, pn), p0, pn))
-                keep_back = 0
-                if gi == 3 and 0 < mine[0][0] and j < len(units) - 1:
-                    keep_back = 1 if mine[0][0] > 512 else 2
+                keep_back = 1 if gi == 3 and j < len(units) - 1 else 0
                 while n_done < len(waiting) - keep_back:
                     og, p0, pn = waiting[n_done]
                     combine(gi, og, p0, pn)

@@ -21,7 +21,7 @@ GH = H // K_PASS
 G = GX + GH
 NT = 512
 NCH = H // NT
-WORD_BUFS = 16
+WORD_BUFS = 12
 LOOKAHEAD = 8
 
 FLOPS = 2 * 128 * (I_DIM + H) * 4 * H
@@ -48,13 +48,13 @@ def tile_lstmcell_w_kernel(
         psum = ctx.enter_context(tc.psum_pool(name="psum", bufs=8))
         ctx.enter_context(tc.manual_schedule())
 
-        planes = keep.tile([P, 8 * H], U8, name="planes", align_bytes=64)
+        planes = keep.tile([P, 8 * H], U8, name="planes", align_bytes=256)
         brow = keep.tile([P, 4 * H], BF16, name="brow")
         ones = keep.tile([P, P], BF16, name="ones")
         ident = keep.tile([P, P], F32, name="ident")
-        x_sb = keep.tile([P, I_DIM], BF16, name="x_sb")
-        h_sb = keep.tile([P, H], BF16, name="h_sb")
-        c_sb = keep.tile([P, H], BF16, name="c_sb")
+        x_sb = keep.tile([P, I_DIM], BF16, name="x_sb", align_bytes=256)
+        h_sb = keep.tile([P, H], BF16, name="h_sb", align_bytes=256)
+        c_sb = keep.tile([P, H], BF16, name="c_sb", align_bytes=256)
         grouped = keep.tile([P, G * K_PASS], BF16, name="grouped", align_bytes=64)
         codes = keep.tile([P, G * P], U32, name="codes", align_bytes=64)
         xplanes = keep.tile([P, G * P], U8, name="xplanes", align_bytes=64)
@@ -95,7 +95,7 @@ def tile_lstmcell_w_kernel(
 
         def load_words(j):
             gi, gs, lo, n = units[j]
-            wt = words.tile([P, H], U32, name="wt", tag="wt", align_bytes=64)
+            wt = words.tile([P, H], U32, name="wt", tag="wt", align_bytes=4096)
             if len(gs) == 1:
                 g = gs[0]
                 src_w = w_words[gi][g] if g < GX else u_words[gi][g - GX]
@@ -189,7 +189,7 @@ def tile_lstmcell_w_kernel(
                 nc.vector.tensor_tensor(out=cg[:, cols], in0=cg[:, cols], in1=fc[:, cols], op=ALU.add)
                 nc.scalar.activation(out=th[:, cols], in_=cg[:, cols], func=ACT.Tanh)
             elif gi == 3:
-                res = work.tile([P, NT], F32, name="res", tag="res")
+                res = work.tile([P, NT], F32, name="res", tag="res", align_bytes=256)
                 nc.vector.tensor_tensor(out=res[:, 0:n], in0=og[:, 0:n], in1=th[:, cols], op=ALU.mult)
                 nc.sync.dma_start(out=out[:, cols], in_=res[:, 0:n])
 

@@ -80,22 +80,22 @@ def tile_lstmcell_w_kernel(
                     in_=sc[:, 4 * q:4 * q + 4, :],
                 )
 
-        for (kind, gi) in (("u", 0), ("u", 1), ("u", 2), ("w", 3), ("u", 3)):
-            load_scales(kind, gi, nc.gpsimd, F32)
+        for gi in range(4):
+            load_scales("u", gi, nc.gpsimd, F32)
 
         units = []
-        for gi in range(4):
+        for gi in range(3):
             for g in range(G):
-                if gi < 3 or g < GX:
-                    units.append((gi, (g,), 0, H))
+                units.append((gi, (g,), 0, H))
         gate_parts = [[(c * NT, NT) for c in range(NCH)] for gi in range(3)] + [[(0, 512), (512, 512), (1024, 256), (1280, 128), (1408, 128)]]
         for (p0, pn) in gate_parts[3]:
+            units.append((3, (0, 1, 2, 3), p0, pn))
             units.append((3, (4, 5, 6), p0, pn))
         wts = {}
 
         def load_words(j):
             gi, gs, lo, n = units[j]
-            wt = words.tile([P, H], U32, name="wt", tag="wt", align_bytes=4096)
+            wt = words.tile([P, 4 * NT], U32, name="wt", tag="wt", align_bytes=4096)
             if len(gs) == 1:
                 g = gs[0]
                 src_w = w_words[gi][g] if g < GX else u_words[gi][g - GX]
@@ -112,7 +112,7 @@ def tile_lstmcell_w_kernel(
             else:
                 nc.sync.dma_start(
                     out=wt[:, 0:len(gs) * n].bitcast(I32).rearrange("p (g n) -> p g n", g=len(gs)),
-                    in_=u_words[gi].rearrange("g p n t -> p g (n t)")[:, :, 4 * lo:4 * (lo + n)].bitcast(I32),
+                    in_=(w_words[gi] if gs[0] < GX else u_words[gi]).rearrange("g p n t -> p g (n t)")[:, :, 4 * lo:4 * (lo + n)].bitcast(I32),
                 )
             wts[j] = wt
 
@@ -126,6 +126,8 @@ def tile_lstmcell_w_kernel(
                     nc.sync.dma_start(out=c_sb[:], in_=c_prev)
                 if j in (3, 7):
                     load_scales("w", (j + 1) // 4, nc.sync, I32)
+                if j == 7:
+                    load_scales("w", 3, nc.sync, I32)
 
         first_loads(0, LOOKAHEAD)
 
@@ -197,11 +199,11 @@ def tile_lstmcell_w_kernel(
         waiting = []
         n_done = 0
         for j, (gi, gs, lo, n) in enumerate(units):
-            if gs[0] == 0:
-                for (p0, pn) in gate_parts[gi]:
-                    accs[(gi, p0)] = psum.tile([P, NT], F32, name="acc%d" % p0, tag="bank")
             wt = wts[j]
             mine = [(p0, pn) for (p0, pn) in gate_parts[gi] if lo <= p0 < lo + n]
+            if gs[0] == 0:
+                for (p0, pn) in mine:
+                    accs[(gi, p0)] = psum.tile([P, NT], F32, name="acc%d" % p0, tag="bank")
             for a, g in enumerate(gs):
                 if g < GX:
                     k = 4 * g
@@ -222,7 +224,7 @@ def tile_lstmcell_w_kernel(
                     )
             if j + LOOKAHEAD < len(units):
                 load_words(j + LOOKAHEAD)
-            if gs[0] == (4 if gi < 3 else 2) and lo == 0:
+            if gs[0] == (4 if gi < 3 else 0) and lo == 0:
                 spread_bias(gi)
             if gs[-1] == G - 1:
                 for (p0, pn) in mine:

@@ -99,16 +99,10 @@ def tile_lstmcell_w_kernel(
             if len(gs) == 1:
                 g = gs[0]
                 src_w = w_words[gi][g] if g < GX else u_words[gi][g - GX]
-                if j % 2 == 0 or j < LOOKAHEAD:
-                    nc.sync.dma_start(
-                        out=wt[:, 0:n].bitcast(I32),
-                        in_=src_w.rearrange("p n t -> p (n t)")[:, 4 * lo:4 * (lo + n)].bitcast(I32),
-                    )
-                else:
-                    nc.scalar.dma_start(
-                        out=wt[:, 0:n].bitcast(F32),
-                        in_=src_w.rearrange("p n t -> p (n t)")[:, 4 * lo:4 * (lo + n)].bitcast(F32),
-                    )
+                nc.sync.dma_start(
+                    out=wt[:, 0:n].bitcast(I32),
+                    in_=src_w.rearrange("p n t -> p (n t)")[:, 4 * lo:4 * (lo + n)].bitcast(I32),
+                )
             else:
                 nc.sync.dma_start(
                     out=wt[:, 0:len(gs) * n].bitcast(I32).rearrange("p (g n) -> p g n", g=len(gs)),

@@ -21,8 +21,8 @@ GH = H // K_PASS
 G = GX + GH
 NT = 512
 NCH = H // NT
-WORD_BUFS = 12
-LOOKAHEAD = 8
+WORD_BUFS = 8
+LOOKAHEAD = 6
 
 FLOPS = 2 * 128 * (I_DIM + H) * 4 * H
 
@@ -85,8 +85,8 @@ def tile_lstmcell_w_kernel(
 
         units = []
         for gi in range(3):
-            for g in range(G):
-                units.append((gi, (g,), 0, H))
+            for gs in ((0, 1), (2, 3), (4, 5), (6,)):
+                units.append((gi, gs, 0, H))
         gate_parts = [[(c * NT, NT) for c in range(NCH)] for gi in range(3)] + [[(0, 512), (512, 512), (1024, 256), (1280, 128), (1408, 128)]]
         for (p0, pn) in gate_parts[3]:
             units.append((3, (0, 1, 2, 3), p0, pn))
@@ -95,7 +95,7 @@ def tile_lstmcell_w_kernel(
 
         def load_words(j):
             gi, gs, lo, n = units[j]
-            wt = words.tile([P, 4 * NT], U32, name="wt", tag="wt", align_bytes=4096)
+            wt = words.tile([P, 2 * H], U32, name="wt", tag="wt", align_bytes=4096)
             if len(gs) == 1:
                 g = gs[0]
                 src_w = w_words[gi][g] if g < GX else u_words[gi][g - GX]
@@ -106,7 +106,7 @@ def tile_lstmcell_w_kernel(
             else:
                 nc.sync.dma_start(
                     out=wt[:, 0:len(gs) * n].bitcast(I32).rearrange("p (g n) -> p g n", g=len(gs)),
-                    in_=(w_words[gi] if gs[0] < GX else u_words[gi]).rearrange("g p n t -> p g (n t)")[:, :, 4 * lo:4 * (lo + n)].bitcast(I32),
+                    in_=(w_words[gi][gs[0]:gs[-1] + 1] if gs[0] < GX else u_words[gi][gs[0] - GX:gs[-1] + 1 - GX]).rearrange("g p n t -> p g (n t)")[:, :, 4 * lo:4 * (lo + n)].bitcast(I32),
                 )
             wts[j] = wt
 
@@ -116,12 +116,10 @@ def tile_lstmcell_w_kernel(
         def first_loads(j0, j1):
             for j in range(j0, j1):
                 load_words(j)
-                if j == 3:
+                if j == 1:
                     nc.sync.dma_start(out=c_sb[:], in_=c_prev)
-                if j in (3, 7):
-                    load_scales("w", (j + 1) // 4, nc.sync, I32)
-                if j == 7:
-                    load_scales("w", 3, nc.sync, I32)
+                if j in (1, 3, 5):
+                    load_scales("w", (j + 1) // 2, nc.sync, I32)
 
         first_loads(0, LOOKAHEAD)
 

@@ -45,7 +45,8 @@ def tile_lstmcell_w_kernel(
         keep = ctx.enter_context(tc.tile_pool(name="keep", bufs=1))
         words = ctx.enter_context(tc.tile_pool(name="words", bufs=WORD_BUFS))
         work = ctx.enter_context(tc.tile_pool(name="work", bufs=5))
-        psum = ctx.enter_context(tc.psum_pool(name="psum", bufs=8))
+        psum = ctx.enter_context(tc.psum_pool(name="psum", bufs=6))
+        psum_bias = ctx.enter_context(tc.psum_pool(name="psum_bias", bufs=2))
         ctx.enter_context(tc.manual_schedule())
 
         planes = keep.tile([P, 8 * H], U8, name="planes", align_bytes=256)
@@ -80,7 +81,9 @@ def tile_lstmcell_w_kernel(
                     in_=sc[:, 4 * q:4 * q + 4, :],
                 )
 
-        for gi in range(4):
+        load_scales("u", 0, nc.gpsimd, F32)
+        for gi in range(1, 4):
+            load_scales("w", gi, nc.gpsimd, F32)
             load_scales("u", gi, nc.gpsimd, F32)
 
         units = []
@@ -118,8 +121,6 @@ def tile_lstmcell_w_kernel(
                 load_words(j)
                 if j == 1:
                     nc.sync.dma_start(out=c_sb[:], in_=c_prev)
-                if j in (1, 3, 5):
-                    load_scales("w", (j + 1) // 2, nc.sync, I32)
 
         first_loads(0, LOOKAHEAD)
 
@@ -155,7 +156,7 @@ def tile_lstmcell_w_kernel(
 
         def spread_bias(gi):
             for cb in range(gi * NCH, (gi + 1) * NCH):
-                bp = psum.tile([P, NT], F32, name="bp", tag="bank")
+                bp = psum_bias.tile([P, NT], F32, name="bp")
                 nc.tensor.matmul(out=bp[:], lhsT=ones[:], rhs=brow[:, cb * NT:(cb + 1) * NT], start=True, stop=True)
                 if cb % 2 == 0:
                     nc.scalar.copy(out=bias_bc[:, cb * NT:(cb + 1) * NT], in_=bp[:])
@@ -216,8 +217,9 @@ def tile_lstmcell_w_kernel(
                     )
             if j + LOOKAHEAD < len(units):
                 load_words(j + LOOKAHEAD)
-            if gs[0] == (4 if gi < 3 else 0) and lo == 0:
-                spread_bias(gi)
+            if gi < 2 and gs[0] == GX:
+                spread_bias(2 * gi)
+                spread_bias(2 * gi + 1)
             if gs[-1] == G - 1:
                 for (p0, pn) in mine:
                     waiting.append((pre_activation(gi, accs[(gi, p0)][:, 0:pn], p0, pn), p0, pn))

@@ -95,21 +95,23 @@ def tile_lstmcell_w_kernel(
             units.append((3, (0, 1, 2, 3), p0, pn))
             units.append((3, (4, 5, 6), p0, pn))
         wts = {}
+        on_scalar = range(1, 12, 2)
 
         def load_words(j):
             gi, gs, lo, n = units[j]
             wt = words.tile([P, 2 * H], U32, name="wt", tag="wt", align_bytes=4096)
+            engine, dt = (nc.scalar, F32) if j in on_scalar else (nc.sync, I32)
             if len(gs) == 1:
                 g = gs[0]
                 src_w = w_words[gi][g] if g < GX else u_words[gi][g - GX]
-                nc.sync.dma_start(
-                    out=wt[:, 0:n].bitcast(I32),
-                    in_=src_w.rearrange("p n t -> p (n t)")[:, 4 * lo:4 * (lo + n)].bitcast(I32),
+                engine.dma_start(
+                    out=wt[:, 0:n].bitcast(dt),
+                    in_=src_w.rearrange("p n t -> p (n t)")[:, 4 * lo:4 * (lo + n)].bitcast(dt),
                 )
             else:
-                nc.sync.dma_start(
-                    out=wt[:, 0:len(gs) * n].bitcast(I32).rearrange("p (g n) -> p g n", g=len(gs)),
-                    in_=(w_words[gi][gs[0]:gs[-1] + 1] if gs[0] < GX else u_words[gi][gs[0] - GX:gs[-1] + 1 - GX]).rearrange("g p n t -> p g (n t)")[:, :, 4 * lo:4 * (lo + n)].bitcast(I32),
+                engine.dma_start(
+                    out=wt[:, 0:len(gs) * n].bitcast(dt).rearrange("p (g n) -> p g n", g=len(gs)),
+                    in_=(w_words[gi][gs[0]:gs[-1] + 1] if gs[0] < GX else u_words[gi][gs[0] - GX:gs[-1] + 1 - GX]).rearrange("g p n t -> p g (n t)")[:, :, 4 * lo:4 * (lo + n)].bitcast(dt),
                 )
             wts[j] = wt
 

from contextlib import ExitStack

import concourse.mybir as mybir
from concourse.masks import make_identity

F32 = mybir.dt.float32
BF16 = mybir.dt.bfloat16
I32 = mybir.dt.int32
U32 = mybir.dt.uint32
U8 = mybir.dt.uint8
FP8X4 = mybir.dt.float8_e4m3fn_x4
ACT = mybir.ActivationFunctionType
ALU = mybir.AluOpType

P = 128
I_DIM = 2048
H = 1536
K_PASS = 512
GX = I_DIM // K_PASS
GH = H // K_PASS
G = GX + GH
NT = 512
NCH = H // NT
WORD_BUFS = 8
LOOKAHEAD = 6

FLOPS = 2 * 128 * (I_DIM + H) * 4 * H


def tile_lstmcell_w_kernel(
    tc, x_t, h_prev, c_prev,
    W_f_words, W_f_scales, W_i_words, W_i_scales, W_c_words, W_c_scales, W_o_words, W_o_scales,
    U_f_words, U_f_scales, U_i_words, U_i_scales, U_c_words, U_c_scales, U_o_words, U_o_scales,
    b_f, b_i, b_c, b_o, out,
):
    nc = tc.nc
    w_words = [W_f_words, W_i_words, W_c_words, W_o_words]
    w_scales = [W_f_scales, W_i_scales, W_c_scales, W_o_scales]
    u_words = [U_f_words, U_i_words, U_c_words, U_o_words]
    u_scales = [U_f_scales, U_i_scales, U_c_scales, U_o_scales]
    biases = [b_f, b_i, b_c, b_o]
    funcs = [ACT.Sigmoid, ACT.Sigmoid, ACT.Tanh, ACT.Sigmoid]

    with ExitStack() as ctx:
        keep = ctx.enter_context(tc.tile_pool(name="keep", bufs=1))
        words = ctx.enter_context(tc.tile_pool(name="words", bufs=WORD_BUFS))
        work = ctx.enter_context(tc.tile_pool(name="work", bufs=5))
        psum = ctx.enter_context(tc.psum_pool(name="psum", bufs=6))
        psum_bias = ctx.enter_context(tc.psum_pool(name="psum_bias", bufs=2))
        ctx.enter_context(tc.manual_schedule())

        planes = keep.tile([P, 8 * H], U8, name="planes", align_bytes=256)
        brow = keep.tile([P, 4 * H], BF16, name="brow")
        ones = keep.tile([P, P], BF16, name="ones")
        ident = keep.tile([P, P], F32, name="ident")
        x_sb = keep.tile([P, I_DIM], BF16, name="x_sb", align_bytes=256)
        h_sb = keep.tile([P, H], BF16, name="h_sb", align_bytes=256)
        c_sb = keep.tile([P, H], BF16, name="c_sb", align_bytes=256)
        grouped = keep.tile([P, G * K_PASS], BF16, name="grouped", align_bytes=64)
        codes = keep.tile([P, G * P], U32, name="codes", align_bytes=64)
        xplanes = keep.tile([P, G * P], U8, name="xplanes", align_bytes=64)
        bias_bc = keep.tile([P, 4 * H], F32, name="bias_bc")
        fc = keep.tile([P, H], F32, name="fc")
        ig = keep.tile([P, H], F32, name="ig")
        cg = keep.tile([P, H], F32, name="cg")
        th = keep.tile([P, H], F32, name="th")

        blocks = {("w", 0): 0, ("u", 0): 1, ("w", 1): 2, ("u", 1): 3, ("w", 2): 4, ("u", 2): 5, ("w", 3): 6, ("u", 3): 7}
        for piece in range(4):
            nc.vector.memset(planes[:, 2 * piece * H:2 * (piece + 1) * H].bitcast(I32), 0)
        nc.vector.memset(ones[:], 1.0)
        make_identity(nc, ident[:])

        def load_scales(kind, gi, engine, dt):
            sc = (w_scales[gi] if kind == "w" else u_scales[gi]).bitcast(dt)
            n_planes = GX if kind == "w" else GH
            base = blocks[(kind, gi)] * H
            for q in (0, 2, 1, 3):
                engine.dma_start(
                    out=planes[32 * q:32 * q + 4 * n_planes, base:base + H].bitcast(dt),
                    in_=sc[:, 4 * q:4 * q + 4, :],
                )

        load_scales("u", 0, nc.gpsimd, F32)
        for gi in range(1, 4):
            load_scales("w", gi, nc.gpsimd, F32)
            load_scales("u", gi, nc.gpsimd, F32)

        units = []
        for gi in range(3):
            for gs in ((0, 1), (2, 3), (4, 5), (6,)):
                units.append((gi, gs, 0, H))
        gate_parts = [[(c * NT, NT) for c in range(NCH)] for gi in range(3)] + [[(0, 512), (512, 512), (1024, 256), (1280, 128), (1408, 128)]]
        for (p0, pn) in gate_parts[3]:
            units.append((3, (0, 1, 2, 3), p0, pn))
            units.append((3, (4, 5, 6), p0, pn))
        wts = {}
        on_scalar = range(1, 12, 2)

        def load_words(j):
            gi, gs, lo, n = units[j]
            wt = words.tile([P, 2 * H], U32, name="wt", tag="wt", align_bytes=4096)
            engine, dt = (nc.scalar, F32) if j in on_scalar else (nc.sync, I32)
            if len(gs) == 1:
                g = gs[0]
                src_w = w_words[gi][g] if g < GX else u_words[gi][g - GX]
                engine.dma_start(
                    out=wt[:, 0:n].bitcast(dt),
                    in_=src_w.rearrange("p n t -> p (n t)")[:, 4 * lo:4 * (lo + n)].bitcast(dt),
                )
            else:
                engine.dma_start(
                    out=wt[:, 0:len(gs) * n].bitcast(dt).rearrange("p (g n) -> p g n", g=len(gs)),
                    in_=(w_words[gi][gs[0]:gs[-1] + 1] if gs[0] < GX else u_words[gi][gs[0] - GX:gs[-1] + 1 - GX]).rearrange("g p n t -> p g (n t)")[:, :, 4 * lo:4 * (lo + n)].bitcast(dt),
                )
            wts[j] = wt

        nc.sync.dma_start(out=x_sb[:], in_=x_t)
        load_scales("w", 0, nc.sync, I32)
        nc.sync.dma_start(out=h_sb[:], in_=h_prev)
        def first_loads(j0, j1):
            for j in range(j0, j1):
                load_words(j)
                if j == 1:
                    nc.sync.dma_start(out=c_sb[:], in_=c_prev)

        first_loads(0, LOOKAHEAD)

        srcs = [(x_sb, g) for g in range(GX)] + [(h_sb, g) for g in range(GH)]
        g32 = grouped[:].bitcast(F32)
        for j in range((G + 1) // 2):
            pair = srcs[2 * j:2 * j + 2]
            n = len(pair)
            xt = psum.tile([P, NT], F32, name="xt", tag="bank")
            for a, (src, g) in enumerate(pair):
                s32 = src[:].bitcast(F32)
                for u in range(2):
                    nc.tensor.transpose(
                        xt[:, (2 * a + u) * P:(2 * a + u + 1) * P],
                        s32[:, 256 * g + u:256 * (g + 1):2],
                        ident[:],
                    )
            dst = g32[:, 512 * j:512 * j + 256 * n].rearrange("p (a b u) -> p a b u", a=n, u=2)
            srcv = xt[:, 0:256 * n].rearrange("p (a u b) -> p a b u", a=n, u=2)
            if j % 2 == 0:
                nc.vector.tensor_copy(out=dst, in_=srcv)
            else:
                nc.scalar.copy(out=dst, in_=srcv)
        for (lo, width) in ((0, 2048), (2048, 1024), (3072, 512)):
            nc.vector.quantize_mx(
                out=codes[:, lo // 4:(lo + width) // 4].bitcast(FP8X4),
                scales=xplanes[:, lo // 4:(lo + width) // 4],
                in_=grouped[:, lo:lo + width],
            )
        nc.vector.memset(brow[:].bitcast(I32), 0)
        for gi in range(4):
            nc.scalar.dma_start(out=brow[0:1, gi * H:(gi + 1) * H], in_=biases[gi].unsqueeze(0))

        def spread_bias(gi):
            for cb in range(gi * NCH, (gi + 1) * NCH):
                bp = psum_bias.tile([P, NT], F32, name="bp")
                nc.tensor.matmul(out=bp[:], lhsT=ones[:], rhs=brow[:, cb * NT:(cb + 1) * NT], start=True, stop=True)
                if cb % 2 == 0:
                    nc.scalar.copy(out=bias_bc[:, cb * NT:(cb + 1) * NT], in_=bp[:])
                else:
                    nc.vector.tensor_copy(out=bias_bc[:, cb * NT:(cb + 1) * NT], in_=bp[:])

        dsts = [fc, ig, cg, None]

        def pre_activation(gi, acc, lo, n):
            z = work.tile([P, NT], F32, name="z", tag="z")
            nc.vector.tensor_tensor(out=z[:, 0:n], in0=acc, in1=bias_bc[:, gi * H + lo:gi * H + lo + n], op=ALU.add)
            if gi < 3:
                nc.scalar.activation(out=dsts[gi][:, lo:lo + n], in_=z[:, 0:n], func=funcs[gi])
                return None
            og = work.tile([P, NT], F32, name="og", tag="og")
            nc.scalar.activation(out=og[:, 0:n], in_=z[:, 0:n], func=funcs[gi])
            return og

        def combine(gi, og, lo, n):
            cols = slice(lo, lo + n)
            if gi == 0:
                nc.vector.tensor_tensor(out=fc[:, cols], in0=fc[:, cols], in1=c_sb[:, cols], op=ALU.mult)
            elif gi == 2:
                nc.vector.tensor_tensor(out=cg[:, cols], in0=cg[:, cols], in1=ig[:, cols], op=ALU.mult)
                nc.vector.tensor_tensor(out=cg[:, cols], in0=cg[:, cols], in1=fc[:, cols], op=ALU.add)
                nc.scalar.activation(out=th[:, cols], in_=cg[:, cols], func=ACT.Tanh)
            elif gi == 3:
                res = work.tile([P, NT], F32, name="res", tag="res", align_bytes=256)
                nc.vector.tensor_tensor(out=res[:, 0:n], in0=og[:, 0:n], in1=th[:, cols], op=ALU.mult)
                nc.sync.dma_start(out=out[:, cols], in_=res[:, 0:n])

        accs = {}
        waiting = []
        n_done = 0
        for j, (gi, gs, lo, n) in enumerate(units):
            wt = wts[j]
            mine = [(p0, pn) for (p0, pn) in gate_parts[gi] if lo <= p0 < lo + n]
            if gs[0] == 0:
                for (p0, pn) in mine:
                    accs[(gi, p0)] = psum.tile([P, NT], F32, name="acc%d" % p0, tag="bank")
            for a, g in enumerate(gs):
                if g < GX:
                    k = 4 * g
                    base = blocks[("w", gi)] * H
                else:
                    k = 4 * (g - GX)
                    base = blocks[("u", gi)] * H
                for (p0, pn) in mine:
                    off = a * n + p0 - lo
                    nc.tensor.matmul_mx(
                        out=accs[(gi, p0)][:, 0:pn],
                        lhsT=codes[:, g * P:(g + 1) * P].bitcast(FP8X4),
                        lhsT_scale=xplanes[:, g * P:(g + 1) * P],
                        rhs=wt[:, off:off + pn].bitcast(FP8X4),
                        rhs_scale=planes[k:P, base + p0:base + p0 + pn],
                        start=(g == 0),
                        stop=(g == G - 1),
                    )
            if j + LOOKAHEAD < len(units):
                load_words(j + LOOKAHEAD)
            if gi < 2 and gs[0] == GX:
                spread_bias(2 * gi)
                spread_bias(2 * gi + 1)
            if gs[-1] == G - 1:
                for (p0, pn) in mine:
                    waiting.append((pre_activation(gi, accs[(gi, p0)][:, 0:pn], p0, pn), p0, pn))
                keep_back = 1 if gi == 3 and j < len(units) - 1 else 0
                while n_done < len(waiting) - keep_back:
                    og, p0, pn = waiting[n_done]
                    combine(gi, og, p0, pn)
                    n_done += 1
